import numpy as np
import ml_dtypes


def mxq(x, axis, fmt="e4m3"):
    dtype, down = {"e4m3": (ml_dtypes.float8_e4m3fn, 7), "e5m2": (ml_dtypes.float8_e5m2, 14)}[fmt]
    v = np.moveaxis(np.asarray(x, np.float32).astype(ml_dtypes.bfloat16).astype(np.float64), axis, -1)
    blocks = v.reshape(v.shape[:-1] + (-1, 32))
    amax = np.abs(blocks).max(-1, keepdims=True)
    byte = np.maximum(np.where(amax > 0, np.frexp(amax)[1] - 1 + 127, 0) - down, 1)
    scale = np.exp2(byte - 127.0)
    codes = (blocks / scale).astype(np.float32).astype(dtype).astype(np.float64)
    return np.moveaxis((codes * scale).reshape(v.shape), -1, axis)


WIDE = False


def mx_kscale(k):
    if not WIDE:
        return np.ones(k)
    levels = np.array([10, -10, 5, -5, 0])
    a = np.random.permutation(np.resize(levels, k // 512 * 4)).reshape(k // 512, 4)
    idx = np.arange(k)
    return np.exp2(a[idx // 512, idx % 128 // 32])


BF16 = ml_dtypes.bfloat16


def bf(x):
    return np.asarray(x, np.float32).astype(BF16)


def f64(x):
    return np.asarray(x).astype(np.float64)


E2M1 = np.array([0.0, 0.5, 1.0, 1.5, 2.0, 3.0, 4.0, 6.0, -0.0, -0.5, -1.0, -1.5, -2.0, -3.0, -4.0, -6.0])


def pack_weight(w, fmt):
    k, n = w.shape
    w = f64(bf(w)).reshape(k // 32, 32, n)
    amax = np.abs(w).max(1)
    if fmt == "e4m3":
        byte = np.frexp(amax)[1] - 1 + 127 - 7
    else:
        mant, ex = np.frexp(amax / 6.0)
        byte = np.where(mant > 0.5, ex, ex - 1) + 127
    byte = np.clip(np.where(amax > 0, byte, 1), 1, 254)
    scaled = (w * np.exp2(127.0 - byte)[:, None, :]).reshape(k, n).astype(np.float32)
    by_word = np.ascontiguousarray(scaled.reshape(k // 512, 128, 4, n).transpose(0, 1, 3, 2))
    if fmt == "e4m3":
        words = by_word.astype(ml_dtypes.float8_e4m3fn).view(np.uint8)
    else:
        c = by_word.astype(ml_dtypes.float4_e2m1fn).view(np.uint8) & 0xF
        words = c[..., 0::2] | (c[..., 1::2] << 4)
    return np.ascontiguousarray(words), np.ascontiguousarray(byte.astype(np.uint8).reshape(k // 512, 16, n))


def unpack_weight(words, scales, fmt):
    g, p, n, _ = words.shape
    if fmt == "e4m3":
        vals = np.ascontiguousarray(words).view(ml_dtypes.float8_e4m3fn).astype(np.float64)
    else:
        nib = np.empty((g, p, n, 4), np.uint8)
        nib[..., 0::2] = words & 0xF
        nib[..., 1::2] = words >> 4
        vals = E2M1[nib]
    vals = vals * np.repeat(np.exp2(scales.astype(np.float64) - 127.0), 8, axis=1)[..., None]
    return vals.transpose(0, 1, 3, 2).reshape(g * 512, n)


B, INPUT_DIM, PE_DIM, OUT_DIM = 128, 32, 16384, 1024
DPI = PE_DIM // INPUT_DIM
MAX_COORD = 10.0
LN_EPS = 1e-5
MXB = 32
J0 = DPI // 2 - 2
LO = J0 // MXB * MXB
FMT = "e4m3"


def sinusoidal_pe(s):
    j = np.arange(DPI, dtype=np.float64)
    freq = np.power(10000.0, -2.0 * j / DPI)
    angle = s[:, :, None] * freq[None, None, :]
    pe = np.where((np.arange(DPI) % 2) == 0, np.sin(angle), np.cos(angle))
    return pe.reshape(s.shape[0], PE_DIM)


def setup_inputs():
    t = mx_kscale(PE_DIM)
    a = 20.0 * float(np.max(t) > np.min(t))
    fac = np.full((INPUT_DIM, DPI), np.exp2(-a / 10))
    fac[:, LO:LO + MXB] = np.exp2(-a / 10 - a / 2)
    fac[:, J0] = np.exp2(a - a / 5)
    fac = fac.reshape(PE_DIM)
    state = bf(np.random.uniform(-0.5, 1.5, (B, INPUT_DIM)) * MAX_COORD)
    w = np.random.standard_normal((OUT_DIM, PE_DIM)) * 0.024 / np.sqrt(PE_DIM) * fac[None, :]
    words, scales = pack_weight(w.T, FMT)
    return {"state": state,
            "W_words": words,
            "W_scales": scales,
            "b": bf((0.01 + 0.01 * np.random.standard_normal(OUT_DIM)) * np.exp2(-a / 10)),
            "gamma": bf(1.0 + 0.1 * np.random.standard_normal(OUT_DIM)),
            "beta": bf(0.1 * np.random.standard_normal(OUT_DIM))}


def reference(state, W_words, W_scales, b, gamma, beta):
    s = np.clip(f64(state) / MAX_COORD, 0.0, 1.0)
    pe = sinusoidal_pe(s)
    y = (mxq(pe, 1, "e4m3") @ unpack_weight(W_words, W_scales, FMT)) + f64(b)
    mu = np.mean(y, axis=-1, keepdims=True)
    var = np.mean(np.square(y - mu), axis=-1, keepdims=True)
    return (y - mu) / np.sqrt(var + LN_EPS) * f64(gamma) + f64(beta)

@@ -1,0 +1,188 @@
+import math
+
+import concourse.masks as masks
+import concourse.mybir as mybir
+
+F32 = mybir.dt.float32
+BF16 = mybir.dt.bfloat16
+I32 = mybir.dt.int32
+U32 = mybir.dt.uint32
+U8 = mybir.dt.uint8
+FP8X4 = mybir.dt.float8_e4m3fn_x4
+ALU = mybir.AluOpType
+ACT = mybir.ActivationFunctionType
+
+P = 128
+PACK = 4
+ROWS = 128
+COORDS = 32
+DPI = P * PACK
+OUT = 1024
+BANK = 512
+HALVES = OUT // BANK
+MAX_COORD = 10.0
+LN_EPS = 1e-5
+INDEX_BITS = 9
+CHUNK = 8
+CHUNKS = COORDS // CHUNK
+CHUNK_COLS = CHUNK * ROWS
+SHARE = 4
+QUADRANTS = 4
+
+FLOPS = 2 * ROWS * COORDS * DPI * OUT
+
+
+def tile_positionencoder_k_kernel(tc, state, W_words, W_scales, b, gamma, beta, out):
+    nc = tc.nc
+    with (
+        tc.tile_pool(name="keep", bufs=1) as keep,
+        tc.tile_pool(name="stage", bufs=2) as stage,
+        tc.psum_pool(name="spread_psum", bufs=CHUNKS) as spread_psum,
+        tc.psum_pool(name="vector_psum", bufs=2) as vector_psum,
+        tc.psum_pool(name="acc_psum", bufs=1) as acc_psum,
+    ):
+        state_sb = keep.tile([ROWS, COORDS], BF16)
+        nc.scalar.dma_start(out=state_sb[:], in_=state)
+
+        vector_rows = keep.tile([P, OUT], BF16)
+        nc.vector.memset(vector_rows[:].bitcast(I32), 0)
+        for i, vector in enumerate((b, gamma, beta)):
+            nc.scalar.dma_start(out=vector_rows[i : i + 1, :], in_=vector.unsqueeze(0))
+
+        w_words = keep.tile([P, COORDS, OUT], U32, align_bytes=64)
+        w_planes = keep.tile([P, COORDS // SHARE, OUT], U8, align_bytes=64)
+        for group in range(COORDS // SHARE):
+            first = SHARE * group
+            nc.vector.memset(w_planes[:, group, :].bitcast(I32), 0)
+            for quadrant in range(QUADRANTS):
+                nc.sync.dma_start(
+                    out=w_planes[32 * quadrant : 32 * quadrant + 4 * SHARE, group, :].bitcast(I32),
+                    in_=W_scales[first : first + SHARE, 4 * quadrant : 4 * quadrant + 4, :].bitcast(I32),
+                )
+            for g in range(first, first + SHARE):
+                nc.sync.dma_start(
+                    out=w_words[:, g, :].bitcast(I32),
+                    in_=W_words[g].rearrange("p n t -> p (n t)").bitcast(I32),
+                )
+
+        identity = keep.tile([P, P], BF16)
+        masks.make_identity(nc, identity[:])
+
+        not_j = keep.tile([P, PACK], I32)
+        nc.gpsimd.iota(not_j[:], pattern=[[-1, PACK]], base=DPI - 1, channel_multiplier=-PACK)
+        cleared = keep.tile([P, INDEX_BITS, PACK], I32)
+        factors = keep.tile([P, INDEX_BITS, PACK], F32)
+        for i in range(INDEX_BITS):
+            ratio = 10000.0 ** (-2.0 * (1 << i) / DPI)
+            nc.vector.tensor_scalar(
+                out=cleared[:, i, :], in0=not_j[:], scalar1=i, scalar2=1,
+                op0=ALU.logical_shift_right, op1=ALU.bitwise_and,
+            )
+            nc.vector.tensor_scalar(
+                out=factors[:, i, :], in0=cleared[:, i, :], scalar1=1.0 - ratio, scalar2=ratio,
+                op0=ALU.mult, op1=ALU.add,
+            )
+        f_of_j = keep.tile([P, PACK], F32)
+        nc.vector.tensor_reduce(
+            out=f_of_j[:], in_=factors[:].rearrange("p i t -> p t i"),
+            axis=mybir.AxisListType.X, op=ALU.mult,
+        )
+        freq = keep.tile([P, PACK], F32)
+        nc.vector.tensor_scalar_mul(out=freq[:], in0=f_of_j[:], scalar1=1.0 / MAX_COORD)
+        phase = keep.tile([P, PACK], F32)
+        nc.vector.tensor_scalar(
+            out=phase[:], in0=cleared[:, 0, :], scalar1=-math.pi / 2, scalar2=math.pi / 2,
+            op0=ALU.mult, op1=ALU.add,
+        )
+        eps = keep.tile([P, 1], F32)
+        nc.vector.tensor_scalar(
+            out=eps[:], in0=cleared[:, 0, 0:1], scalar1=0.0, scalar2=LN_EPS,
+            op0=ALU.mult, op1=ALU.add,
+        )
+
+        clipped = keep.tile([ROWS, COORDS], BF16)
+        nc.vector.tensor_scalar(
+            out=clipped[:], in0=state_sb[:], scalar1=0.0, scalar2=MAX_COORD,
+            op0=ALU.max, op1=ALU.min,
+        )
+        pe_codes = keep.tile([P, COORDS * ROWS], U32, align_bytes=64)
+        pe_scales = keep.tile([P, COORDS * ROWS], U8, align_bytes=64)
+        for chunk in range(CHUNKS):
+            spread = spread_psum.tile([P, CHUNK, ROWS], BF16)
+            for i in range(CHUNK):
+                c = CHUNK * chunk + i
+                nc.tensor.matmul(
+                    out=spread[:, i, :], lhsT=clipped[:, c : c + 1].to_broadcast([ROWS, P]),
+                    rhs=identity[:], start=True, stop=True,
+                )
+            planes = stage.tile([P, PACK, CHUNK_COLS], BF16)
+            for t in range(PACK):
+                nc.scalar.activation(
+                    out=planes[:, t, :], in_=spread[:].rearrange("p i r -> p (i r)"), func=ACT.Sin,
+                    bias=phase[:, t : t + 1], scale=freq[:, t : t + 1],
+                )
+            grouped = stage.tile([P, CHUNK_COLS, PACK], BF16, align_bytes=64)
+            nc.vector.tensor_copy(out=grouped[:], in_=planes[:].rearrange("p t w -> p w t"))
+            cols = slice(CHUNK_COLS * chunk, CHUNK_COLS * (chunk + 1))
+            nc.vector.quantize_mx(
+                out=pe_codes[:, cols].bitcast(FP8X4), scales=pe_scales[:, cols],
+                in_=grouped[:].rearrange("p w t -> p (w t)"),
+            )
+        table_warmer = keep.tile([P, 1], F32)
+        nc.scalar.activation(
+            out=table_warmer[:], in_=planes[:, PACK - 1, 0:1], func=ACT.Sqrt, bias=eps[:], scale=0.0,
+        )
+
+        vectors = keep.tile([P, 3, OUT], BF16)
+        for i in range(3):
+            picked = vector_psum.tile([P, OUT], BF16)
+            for half in range(HALVES):
+                cols = slice(BANK * half, BANK * (half + 1))
+                nc.tensor.matmul(
+                    out=picked[:, cols], lhsT=identity[:, i : i + 1].to_broadcast([P, P]),
+                    rhs=vector_rows[:, cols], start=True, stop=True,
+                )
+            nc.vector.tensor_copy(out=vectors[:, i, :], in_=picked[:])
+        b_all, gamma_all, beta_all = vectors[:, 0, :], vectors[:, 1, :], vectors[:, 2, :]
+
+        acc = [acc_psum.tile([ROWS, BANK], F32, name="acc%d" % half) for half in range(HALVES)]
+        for g in range(COORDS):
+            group, place = divmod(g, SHARE)
+            rows = slice(ROWS * g, ROWS * (g + 1))
+            for half in range(HALVES):
+                cols = slice(BANK * half, BANK * (half + 1))
+                nc.tensor.matmul_mx(
+                    out=acc[half][:],
+                    lhsT=pe_codes[:, rows].bitcast(FP8X4),
+                    lhsT_scale=pe_scales[:, rows],
+                    rhs=w_words[:, g, cols].bitcast(FP8X4),
+                    rhs_scale=w_planes[4 * place : P, group, cols],
+                    start=(g == 0),
+                    stop=(g == COORDS - 1),
+                )
+
+        y = keep.tile([ROWS, OUT], F32)
+        stats = keep.tile([ROWS, HALVES, 6], F32)
+        for half in range(HALVES):
+            cols = slice(BANK * half, BANK * (half + 1))
+            nc.vector.tensor_tensor(out=y[:, cols], in0=acc[half][:], in1=b_all[:, cols], op=ALU.add)
+            nc.vector.bn_stats(out=stats[:, half, :], in_=y[:, cols])
+        mean_var = keep.tile([ROWS, 2], F32)
+        nc.vector.bn_aggr(out=mean_var[:], in_=stats[:].rearrange("p h s -> p (h s)"))
+        std = keep.tile([ROWS, 1], F32)
+        nc.scalar.activation(out=std[:], in_=mean_var[:, 1:2], func=ACT.Sqrt, bias=eps[:], scale=1.0)
+        centred = keep.tile([ROWS, OUT], F32)
+        nc.vector.scalar_tensor_tensor(
+            out=centred[:], in0=y[:], scalar=mean_var[:, 0:1], in1=gamma_all,
+            op0=ALU.subtract, op1=ALU.mult,
+        )
+        rstd = keep.tile([ROWS, 1], F32)
+        nc.vector.reciprocal(out=rstd[:], in_=std[:])
+        result = keep.tile([ROWS, OUT], F32)
+        for half in range(HALVES):
+            cols = slice(BANK * half, BANK * (half + 1))
+            nc.vector.scalar_tensor_tensor(
+                out=result[:, cols], in0=centred[:, cols], scalar=rstd[:], in1=beta_all[:, cols],
+                op0=ALU.mult, op1=ALU.add,
+            )
+            nc.sync.dma_start(out=out[:, cols], in_=result[:, cols])

@@ -41,6 +41,8 @@ def tile_positionencoder_k_kernel(tc, state, W_words, W_scales, b, gamma, beta, 
         tc.psum_pool(name="vector_psum", bufs=2) as vector_psum,
         tc.psum_pool(name="acc_psum", bufs=1) as acc_psum,
     ):
+        w_planes = keep.tile([P, COORDS // SHARE, OUT], U8, align_bytes=64)
+        nc.vector.memset(w_planes[:].rearrange("p G n -> p (G n)").bitcast(I32), 0)
         state_sb = keep.tile([ROWS, COORDS], BF16)
         nc.scalar.dma_start(out=state_sb[:], in_=state)
 
@@ -50,26 +52,25 @@ def tile_positionencoder_k_kernel(tc, state, W_words, W_scales, b, gamma, beta, 
             nc.scalar.dma_start(out=vector_rows[i : i + 1, :], in_=vector.unsqueeze(0))
 
         w_words = keep.tile([P, COORDS, OUT], U32, align_bytes=64)
-        w_planes = keep.tile([P, COORDS // SHARE, OUT], U8, align_bytes=64)
-        for group in range(COORDS // SHARE):
-            first = SHARE * group
-            nc.vector.memset(w_planes[:, group, :].bitcast(I32), 0)
-            for quadrant in range(QUADRANTS):
-                nc.sync.dma_start(
-                    out=w_planes[32 * quadrant : 32 * quadrant + 4 * SHARE, group, :].bitcast(I32),
-                    in_=W_scales[first : first + SHARE, 4 * quadrant : 4 * quadrant + 4, :].bitcast(I32),
-                )
-            for g in range(first, first + SHARE):
-                nc.sync.dma_start(
-                    out=w_words[:, g, :].bitcast(I32),
-                    in_=W_words[g].rearrange("p n t -> p (n t)").bitcast(I32),
-                )
+        for g in range(COORDS):
+            nc.sync.dma_start(
+                out=w_words[:, g, :].bitcast(I32),
+                in_=W_words[g].rearrange("p n t -> p (n t)").bitcast(I32),
+            )
 
         identity = keep.tile([P, P], BF16)
         masks.make_identity(nc, identity[:])
-
         not_j = keep.tile([P, PACK], I32)
         nc.gpsimd.iota(not_j[:], pattern=[[-1, PACK]], base=DPI - 1, channel_multiplier=-PACK)
+
+        scale_rows = W_scales.rearrange("(G i) q n -> q i G n", i=SHARE)
+        for q in range(QUADRANTS * 4):
+            first = 32 * (q // 4) + q % 4
+            nc.gpsimd.dma_start(
+                out=w_planes[first : first + 4 * SHARE : 4, :, :].bitcast(F32),
+                in_=scale_rows[q].bitcast(F32),
+            )
+
         cleared = keep.tile([P, INDEX_BITS, PACK], I32)
         factors = keep.tile([P, INDEX_BITS, PACK], F32)
         for i in range(INDEX_BITS):

@@ -27,7 +27,10 @@ CHUNK = 8
 CHUNKS = COORDS // CHUNK
 CHUNK_COLS = CHUNK * ROWS
 SHARE = 4
+GROUPS = COORDS // SHARE
 QUADRANTS = 4
+SYNC_GROUPS = GROUPS // 2
+LATE = 2
 
 FLOPS = 2 * ROWS * COORDS * DPI * OUT
 
@@ -41,8 +44,11 @@ def tile_positionencoder_k_kernel(tc, state, W_words, W_scales, b, gamma, beta, 
         tc.psum_pool(name="vector_psum", bufs=2) as vector_psum,
         tc.psum_pool(name="acc_psum", bufs=1) as acc_psum,
     ):
-        w_planes = keep.tile([P, COORDS // SHARE, OUT], U8, align_bytes=64)
-        nc.vector.memset(w_planes[:].rearrange("p G n -> p (G n)").bitcast(I32), 0)
+        identity = keep.tile([P, P], BF16)
+        masks.make_identity(nc, identity[:])
+        not_j = keep.tile([P, PACK], I32)
+        nc.gpsimd.iota(not_j[:], pattern=[[-1, PACK]], base=DPI - 1, channel_multiplier=-PACK)
+
         state_sb = keep.tile([ROWS, COORDS], BF16)
         nc.scalar.dma_start(out=state_sb[:], in_=state)
 
@@ -52,23 +58,33 @@ def tile_positionencoder_k_kernel(tc, state, W_words, W_scales, b, gamma, beta, 
             nc.scalar.dma_start(out=vector_rows[i : i + 1, :], in_=vector.unsqueeze(0))
 
         w_words = keep.tile([P, COORDS, OUT], U32, align_bytes=64)
-        for g in range(COORDS):
+        w_planes = keep.tile([P, GROUPS, OUT], U8, align_bytes=64)
+
+        def load_scale_rows(queue, view, group):
+            first = SHARE * group
+            for quadrant in range(QUADRANTS):
+                queue.dma_start(
+                    out=w_planes[32 * quadrant : 32 * quadrant + 4 * SHARE, group, :].bitcast(view),
+                    in_=W_scales[first : first + SHARE, 4 * quadrant : 4 * quadrant + 4, :].bitcast(view),
+                )
+
+        for group in range(GROUPS):
+            nc.vector.memset(w_planes[:, group, :].bitcast(I32), 0)
+        for group in range(SYNC_GROUPS, GROUPS):
+            load_scale_rows(nc.gpsimd, F32, group)
+        for group in range(GROUPS):
+            if group < SYNC_GROUPS:
+                load_scale_rows(nc.sync, I32, group)
+            for g in range(SHARE * group, min(SHARE * (group + 1), COORDS - LATE)):
+                nc.sync.dma_start(
+                    out=w_words[:, g, :].bitcast(I32),
+                    in_=W_words[g].rearrange("p n t -> p (n t)").bitcast(I32),
+                )
+        late_words = W_words[COORDS - LATE : COORDS].rearrange("g p n t -> p g (n t)").bitcast(I32)
+        for half in range(HALVES):
+            cols = slice(BANK * half, BANK * (half + 1))
             nc.sync.dma_start(
-                out=w_words[:, g, :].bitcast(I32),
-                in_=W_words[g].rearrange("p n t -> p (n t)").bitcast(I32),
-            )
-
-        identity = keep.tile([P, P], BF16)
-        masks.make_identity(nc, identity[:])
-        not_j = keep.tile([P, PACK], I32)
-        nc.gpsimd.iota(not_j[:], pattern=[[-1, PACK]], base=DPI - 1, channel_multiplier=-PACK)
-
-        scale_rows = W_scales.rearrange("(G i) q n -> q i G n", i=SHARE)
-        for q in range(QUADRANTS * 4):
-            first = 32 * (q // 4) + q % 4
-            nc.gpsimd.dma_start(
-                out=w_planes[first : first + 4 * SHARE : 4, :, :].bitcast(F32),
-                in_=scale_rows[q].bitcast(F32),
+                out=w_words[:, COORDS - LATE : COORDS, cols].bitcast(I32), in_=late_words[:, :, cols]
             )
 
         cleared = keep.tile([P, INDEX_BITS, PACK], I32)
@@ -147,35 +163,63 @@ def tile_positionencoder_k_kernel(tc, state, W_words, W_scales, b, gamma, beta, 
         b_all, gamma_all, beta_all = vectors[:, 0, :], vectors[:, 1, :], vectors[:, 2, :]
 
         acc = [acc_psum.tile([ROWS, BANK], F32, name="acc%d" % half) for half in range(HALVES)]
-        for g in range(COORDS):
+        early = [(g, half) for g in range(COORDS - LATE) for half in range(HALVES)]
+        late = [(g, half) for half in range(HALVES) for g in range(COORDS - LATE, COORDS)]
+        for g, half in early + late:
             group, place = divmod(g, SHARE)
             rows = slice(ROWS * g, ROWS * (g + 1))
-            for half in range(HALVES):
-                cols = slice(BANK * half, BANK * (half + 1))
-                nc.tensor.matmul_mx(
-                    out=acc[half][:],
-                    lhsT=pe_codes[:, rows].bitcast(FP8X4),
-                    lhsT_scale=pe_scales[:, rows],
-                    rhs=w_words[:, g, cols].bitcast(FP8X4),
-                    rhs_scale=w_planes[4 * place : P, group, cols],
-                    start=(g == 0),
-                    stop=(g == COORDS - 1),
-                )
+            cols = slice(BANK * half, BANK * (half + 1))
+            nc.tensor.matmul_mx(
+                out=acc[half][:],
+                lhsT=pe_codes[:, rows].bitcast(FP8X4),
+                lhsT_scale=pe_scales[:, rows],
+                rhs=w_words[:, g, cols].bitcast(FP8X4),
+                rhs_scale=w_planes[4 * place : P, group, cols],
+                start=(g == 0),
+                stop=(g == COORDS - 1),
+            )
 
         y = keep.tile([ROWS, OUT], F32)
-        stats = keep.tile([ROWS, HALVES, 6], F32)
+        squares = keep.tile([ROWS, OUT], F32)
+        sums = keep.tile([ROWS, HALVES], F32)
+        square_sums = [keep.tile([ROWS, 1], F32, name="square_sum%d" % half) for half in range(HALVES)]
+        minus_shift = keep.tile([ROWS, 1], F32)
         for half in range(HALVES):
             cols = slice(BANK * half, BANK * (half + 1))
-            nc.vector.tensor_tensor(out=y[:, cols], in0=acc[half][:], in1=b_all[:, cols], op=ALU.add)
-            nc.vector.bn_stats(out=stats[:, half, :], in_=y[:, cols])
-        mean_var = keep.tile([ROWS, 2], F32)
-        nc.vector.bn_aggr(out=mean_var[:], in_=stats[:].rearrange("p h s -> p (h s)"))
-        std = keep.tile([ROWS, 1], F32)
-        nc.scalar.activation(out=std[:], in_=mean_var[:, 1:2], func=ACT.Sqrt, bias=eps[:], scale=1.0)
+            nc.vector.scalar_tensor_tensor(
+                out=y[:, cols], in0=acc[half][:], scalar=1.0, in1=b_all[:, cols],
+                op0=ALU.mult, op1=ALU.add, accum_out=sums[:, half : half + 1],
+            )
+            if half == 0:
+                nc.vector.tensor_scalar_mul(out=minus_shift[:], in0=sums[:, 0:1], scalar1=-1.0 / BANK)
+            nc.scalar.activation(
+                out=squares[:, cols], in_=y[:, cols], func=ACT.Square, bias=minus_shift[:], scale=1.0,
+                accum_out=square_sums[half][:],
+            )
+        mean = keep.tile([ROWS, 1], F32)
+        nc.vector.tensor_scalar(
+            out=mean[:], in0=sums[:, 0:1], scalar1=sums[:, 1:2], scalar2=1.0 / OUT,
+            op0=ALU.add, op1=ALU.mult,
+        )
         centred = keep.tile([ROWS, OUT], F32)
         nc.vector.scalar_tensor_tensor(
-            out=centred[:], in0=y[:], scalar=mean_var[:, 0:1], in1=gamma_all,
-            op0=ALU.subtract, op1=ALU.mult,
+            out=centred[:], in0=y[:], scalar=mean[:], in1=gamma_all, op0=ALU.subtract, op1=ALU.mult,
+        )
+        first_term = keep.tile([ROWS, 1], F32)
+        nc.scalar.activation(
+            out=first_term[:], in_=square_sums[0][:], func=ACT.Identity, bias=eps[:], scale=1.0 / OUT,
+        )
+        offset_squared = keep.tile([ROWS, 1], F32)
+        nc.scalar.activation(
+            out=offset_squared[:], in_=mean[:], func=ACT.Square, bias=minus_shift[:], scale=1.0,
+        )
+        other_terms = keep.tile([ROWS, 1], F32)
+        nc.scalar.activation(
+            out=other_terms[:], in_=offset_squared[:], func=ACT.Identity, bias=first_term[:], scale=-1.0,
+        )
+        std = keep.tile([ROWS, 1], F32)
+        nc.scalar.activation(
+            out=std[:], in_=square_sums[1][:], func=ACT.Sqrt, bias=other_terms[:], scale=1.0 / OUT,
         )
         rstd = keep.tile([ROWS, 1], F32)
         nc.vector.reciprocal(out=rstd[:], in_=std[:])

@@ -26,10 +26,10 @@ INDEX_BITS = 9
 CHUNK = 8
 CHUNKS = COORDS // CHUNK
 CHUNK_COLS = CHUNK * ROWS
+PIECE_COLS = CHUNK_COLS // 2
 SHARE = 4
 GROUPS = COORDS // SHARE
 QUADRANTS = 4
-SYNC_GROUPS = GROUPS // 2
 LATE = 2
 
 FLOPS = 2 * ROWS * COORDS * DPI * OUT
@@ -39,7 +39,7 @@ def tile_positionencoder_k_kernel(tc, state, W_words, W_scales, b, gamma, beta, 
     nc = tc.nc
     with (
         tc.tile_pool(name="keep", bufs=1) as keep,
-        tc.tile_pool(name="stage", bufs=2) as stage,
+        tc.tile_pool(name="plane_pool", bufs=CHUNKS) as plane_pool,
         tc.psum_pool(name="spread_psum", bufs=CHUNKS) as spread_psum,
         tc.psum_pool(name="vector_psum", bufs=2) as vector_psum,
         tc.psum_pool(name="acc_psum", bufs=1) as acc_psum,
@@ -52,34 +52,27 @@ def tile_positionencoder_k_kernel(tc, state, W_words, W_scales, b, gamma, beta, 
         state_sb = keep.tile([ROWS, COORDS], BF16)
         nc.scalar.dma_start(out=state_sb[:], in_=state)
 
+        w_planes = keep.tile([P, GROUPS, OUT], U8, align_bytes=64)
+        nc.vector.memset(w_planes[:].rearrange("p G n -> p (G n)").bitcast(I32), 0)
+        scale_rows = W_scales.rearrange("(G i) q n -> q i G n", i=SHARE)
+        for q in range(4 * QUADRANTS):
+            first = 32 * (q // 4) + q % 4
+            nc.gpsimd.dma_start(
+                out=w_planes[first : first + 4 * SHARE : 4, :, :].bitcast(F32),
+                in_=scale_rows[q].bitcast(F32),
+            )
+
         vector_rows = keep.tile([P, OUT], BF16)
         nc.vector.memset(vector_rows[:].bitcast(I32), 0)
         for i, vector in enumerate((b, gamma, beta)):
             nc.scalar.dma_start(out=vector_rows[i : i + 1, :], in_=vector.unsqueeze(0))
 
         w_words = keep.tile([P, COORDS, OUT], U32, align_bytes=64)
-        w_planes = keep.tile([P, GROUPS, OUT], U8, align_bytes=64)
-
-        def load_scale_rows(queue, view, group):
-            first = SHARE * group
-            for quadrant in range(QUADRANTS):
-                queue.dma_start(
-                    out=w_planes[32 * quadrant : 32 * quadrant + 4 * SHARE, group, :].bitcast(view),
-                    in_=W_scales[first : first + SHARE, 4 * quadrant : 4 * quadrant + 4, :].bitcast(view),
-                )
-
-        for group in range(GROUPS):
-            nc.vector.memset(w_planes[:, group, :].bitcast(I32), 0)
-        for group in range(SYNC_GROUPS, GROUPS):
-            load_scale_rows(nc.gpsimd, F32, group)
-        for group in range(GROUPS):
-            if group < SYNC_GROUPS:
-                load_scale_rows(nc.sync, I32, group)
-            for g in range(SHARE * group, min(SHARE * (group + 1), COORDS - LATE)):
-                nc.sync.dma_start(
-                    out=w_words[:, g, :].bitcast(I32),
-                    in_=W_words[g].rearrange("p n t -> p (n t)").bitcast(I32),
-                )
+        for g in range(COORDS - LATE):
+            nc.sync.dma_start(
+                out=w_words[:, g, :].bitcast(I32),
+                in_=W_words[g].rearrange("p n t -> p (n t)").bitcast(I32),
+            )
         late_words = W_words[COORDS - LATE : COORDS].rearrange("g p n t -> p g (n t)").bitcast(I32)
         for half in range(HALVES):
             cols = slice(BANK * half, BANK * (half + 1))
@@ -132,19 +125,26 @@ def tile_positionencoder_k_kernel(tc, state, W_words, W_scales, b, gamma, beta, 
                     out=spread[:, i, :], lhsT=clipped[:, c : c + 1].to_broadcast([ROWS, P]),
                     rhs=identity[:], start=True, stop=True,
                 )
-            planes = stage.tile([P, PACK, CHUNK_COLS], BF16)
+            planes = plane_pool.tile([P, PACK, CHUNK_COLS], BF16)
             for t in range(PACK):
                 nc.scalar.activation(
                     out=planes[:, t, :], in_=spread[:].rearrange("p i r -> p (i r)"), func=ACT.Sin,
                     bias=phase[:, t : t + 1], scale=freq[:, t : t + 1],
                 )
-            grouped = stage.tile([P, CHUNK_COLS, PACK], BF16, align_bytes=64)
-            nc.vector.tensor_copy(out=grouped[:], in_=planes[:].rearrange("p t w -> p w t"))
-            cols = slice(CHUNK_COLS * chunk, CHUNK_COLS * (chunk + 1))
-            nc.vector.quantize_mx(
-                out=pe_codes[:, cols].bitcast(FP8X4), scales=pe_scales[:, cols],
-                in_=grouped[:].rearrange("p w t -> p (w t)"),
-            )
+            for piece in range(CHUNK_COLS // PIECE_COLS):
+                grouped = keep.tile([P, PIECE_COLS, PACK], BF16, align_bytes=64)
+                if chunk == 0 and piece == 0:
+                    nc.vector.tensor_copy(
+                        out=grouped[:, 0, 0:2].bitcast(I32), in_=w_planes[:, GROUPS - 1, 0:4].bitcast(I32)
+                    )
+                part = slice(PIECE_COLS * piece, PIECE_COLS * (piece + 1))
+                nc.vector.tensor_copy(out=grouped[:], in_=planes[:, :, part].rearrange("p t w -> p w t"))
+                first = CHUNK_COLS * chunk + PIECE_COLS * piece
+                nc.vector.quantize_mx(
+                    out=pe_codes[:, first : first + PIECE_COLS].bitcast(FP8X4),
+                    scales=pe_scales[:, first : first + PIECE_COLS],
+                    in_=grouped[:].rearrange("p w t -> p (w t)"),
+                )
         table_warmer = keep.tile([P, 1], F32)
         nc.scalar.activation(
             out=table_warmer[:], in_=planes[:, PACK - 1, 0:1], func=ACT.Sqrt, bias=eps[:], scale=0.0,

@@ -26,10 +26,10 @@ INDEX_BITS = 9
 CHUNK = 8
 CHUNKS = COORDS // CHUNK
 CHUNK_COLS = CHUNK * ROWS
-PIECE_COLS = CHUNK_COLS // 2
 SHARE = 4
 GROUPS = COORDS // SHARE
 QUADRANTS = 4
+SYNC_GROUPS = 5
 LATE = 2
 
 FLOPS = 2 * ROWS * COORDS * DPI * OUT
@@ -39,7 +39,7 @@ def tile_positionencoder_k_kernel(tc, state, W_words, W_scales, b, gamma, beta, 
     nc = tc.nc
     with (
         tc.tile_pool(name="keep", bufs=1) as keep,
-        tc.tile_pool(name="plane_pool", bufs=CHUNKS) as plane_pool,
+        tc.tile_pool(name="stage", bufs=2) as stage,
         tc.psum_pool(name="spread_psum", bufs=CHUNKS) as spread_psum,
         tc.psum_pool(name="vector_psum", bufs=2) as vector_psum,
         tc.psum_pool(name="acc_psum", bufs=1) as acc_psum,
@@ -52,27 +52,34 @@ def tile_positionencoder_k_kernel(tc, state, W_words, W_scales, b, gamma, beta, 
         state_sb = keep.tile([ROWS, COORDS], BF16)
         nc.scalar.dma_start(out=state_sb[:], in_=state)
 
-        w_planes = keep.tile([P, GROUPS, OUT], U8, align_bytes=64)
-        nc.vector.memset(w_planes[:].rearrange("p G n -> p (G n)").bitcast(I32), 0)
-        scale_rows = W_scales.rearrange("(G i) q n -> q i G n", i=SHARE)
-        for q in range(4 * QUADRANTS):
-            first = 32 * (q // 4) + q % 4
-            nc.gpsimd.dma_start(
-                out=w_planes[first : first + 4 * SHARE : 4, :, :].bitcast(F32),
-                in_=scale_rows[q].bitcast(F32),
-            )
-
         vector_rows = keep.tile([P, OUT], BF16)
         nc.vector.memset(vector_rows[:].bitcast(I32), 0)
         for i, vector in enumerate((b, gamma, beta)):
             nc.scalar.dma_start(out=vector_rows[i : i + 1, :], in_=vector.unsqueeze(0))
 
         w_words = keep.tile([P, COORDS, OUT], U32, align_bytes=64)
-        for g in range(COORDS - LATE):
-            nc.sync.dma_start(
-                out=w_words[:, g, :].bitcast(I32),
-                in_=W_words[g].rearrange("p n t -> p (n t)").bitcast(I32),
-            )
+        w_planes = keep.tile([P, GROUPS, OUT], U8, align_bytes=64)
+
+        def load_scale_rows(queue, view, group):
+            first = SHARE * group
+            for quadrant in range(QUADRANTS):
+                queue.dma_start(
+                    out=w_planes[32 * quadrant : 32 * quadrant + 4 * SHARE, group, :].bitcast(view),
+                    in_=W_scales[first : first + SHARE, 4 * quadrant : 4 * quadrant + 4, :].bitcast(view),
+                )
+
+        for group in range(GROUPS):
+            nc.vector.memset(w_planes[:, group, :].bitcast(I32), 0)
+        for group in range(SYNC_GROUPS, GROUPS):
+            load_scale_rows(nc.gpsimd, F32, group)
+        for group in range(GROUPS):
+            if group < SYNC_GROUPS:
+                load_scale_rows(nc.sync, I32, group)
+            for g in range(SHARE * group, min(SHARE * (group + 1), COORDS - LATE)):
+                nc.sync.dma_start(
+                    out=w_words[:, g, :].bitcast(I32),
+                    in_=W_words[g].rearrange("p n t -> p (n t)").bitcast(I32),
+                )
         late_words = W_words[COORDS - LATE : COORDS].rearrange("g p n t -> p g (n t)").bitcast(I32)
         for half in range(HALVES):
             cols = slice(BANK * half, BANK * (half + 1))
@@ -125,26 +132,19 @@ def tile_positionencoder_k_kernel(tc, state, W_words, W_scales, b, gamma, beta, 
                     out=spread[:, i, :], lhsT=clipped[:, c : c + 1].to_broadcast([ROWS, P]),
                     rhs=identity[:], start=True, stop=True,
                 )
-            planes = plane_pool.tile([P, PACK, CHUNK_COLS], BF16)
+            planes = stage.tile([P, PACK, CHUNK_COLS], BF16)
             for t in range(PACK):
                 nc.scalar.activation(
                     out=planes[:, t, :], in_=spread[:].rearrange("p i r -> p (i r)"), func=ACT.Sin,
                     bias=phase[:, t : t + 1], scale=freq[:, t : t + 1],
                 )
-            for piece in range(CHUNK_COLS // PIECE_COLS):
-                grouped = keep.tile([P, PIECE_COLS, PACK], BF16, align_bytes=64)
-                if chunk == 0 and piece == 0:
-                    nc.vector.tensor_copy(
-                        out=grouped[:, 0, 0:2].bitcast(I32), in_=w_planes[:, GROUPS - 1, 0:4].bitcast(I32)
-                    )
-                part = slice(PIECE_COLS * piece, PIECE_COLS * (piece + 1))
-                nc.vector.tensor_copy(out=grouped[:], in_=planes[:, :, part].rearrange("p t w -> p w t"))
-                first = CHUNK_COLS * chunk + PIECE_COLS * piece
-                nc.vector.quantize_mx(
-                    out=pe_codes[:, first : first + PIECE_COLS].bitcast(FP8X4),
-                    scales=pe_scales[:, first : first + PIECE_COLS],
-                    in_=grouped[:].rearrange("p w t -> p (w t)"),
-                )
+            grouped = stage.tile([P, CHUNK_COLS, PACK], BF16, align_bytes=64)
+            nc.vector.tensor_copy(out=grouped[:], in_=planes[:].rearrange("p t w -> p w t"))
+            cols = slice(CHUNK_COLS * chunk, CHUNK_COLS * (chunk + 1))
+            nc.vector.quantize_mx(
+                out=pe_codes[:, cols].bitcast(FP8X4), scales=pe_scales[:, cols],
+                in_=grouped[:].rearrange("p w t -> p (w t)"),
+            )
         table_warmer = keep.tile([P, 1], F32)
         nc.scalar.activation(
             out=table_warmer[:], in_=planes[:, PACK - 1, 0:1], func=ACT.Sqrt, bias=eps[:], scale=0.0,

@@ -52,10 +52,10 @@ def tile_positionencoder_k_kernel(tc, state, W_words, W_scales, b, gamma, beta, 
         state_sb = keep.tile([ROWS, COORDS], BF16)
         nc.scalar.dma_start(out=state_sb[:], in_=state)
 
-        vector_rows = keep.tile([P, OUT], BF16)
-        nc.vector.memset(vector_rows[:].bitcast(I32), 0)
-        for i, vector in enumerate((b, gamma, beta)):
-            nc.scalar.dma_start(out=vector_rows[i : i + 1, :], in_=vector.unsqueeze(0))
+        zero = keep.tile([P, 1], F32)
+        nc.vector.memset(zero[:], 0.0)
+        sin_warmer = keep.tile([P, 1], F32)
+        nc.scalar.activation(out=sin_warmer[:], in_=zero[:], func=ACT.Sin)
 
         w_words = keep.tile([P, COORDS, OUT], U32, align_bytes=64)
         w_planes = keep.tile([P, GROUPS, OUT], U8, align_bytes=64)
@@ -68,18 +68,23 @@ def tile_positionencoder_k_kernel(tc, state, W_words, W_scales, b, gamma, beta, 
                     in_=W_scales[first : first + SHARE, 4 * quadrant : 4 * quadrant + 4, :].bitcast(view),
                 )
 
-        for group in range(GROUPS):
+        for group in [0, *range(SYNC_GROUPS, GROUPS), *range(1, SYNC_GROUPS)]:
             nc.vector.memset(w_planes[:, group, :].bitcast(I32), 0)
+        vector_rows = keep.tile([P, OUT], BF16)
+        nc.vector.memset(vector_rows[:].bitcast(I32), 0)
         for group in range(SYNC_GROUPS, GROUPS):
             load_scale_rows(nc.gpsimd, F32, group)
         for group in range(GROUPS):
-            if group < SYNC_GROUPS:
-                load_scale_rows(nc.sync, I32, group)
             for g in range(SHARE * group, min(SHARE * (group + 1), COORDS - LATE)):
                 nc.sync.dma_start(
                     out=w_words[:, g, :].bitcast(I32),
                     in_=W_words[g].rearrange("p n t -> p (n t)").bitcast(I32),
                 )
+                if g == SHARE * group and group < SYNC_GROUPS:
+                    load_scale_rows(nc.sync, I32, group)
+                if g == 2:
+                    for i, vector in enumerate((b, gamma, beta)):
+                        nc.sync.dma_start(out=vector_rows[i : i + 1, :], in_=vector.unsqueeze(0))
         late_words = W_words[COORDS - LATE : COORDS].rearrange("g p n t -> p g (n t)").bitcast(I32)
         for half in range(HALVES):
             cols = slice(BANK * half, BANK * (half + 1))

@@ -20,6 +20,7 @@ DPI = P * PACK
 OUT = 1024
 BANK = 512
 HALVES = OUT // BANK
+CHUNK_WIDTHS = (512, 256, 256)
 MAX_COORD = 10.0
 LN_EPS = 1e-5
 INDEX_BITS = 9
@@ -30,17 +31,21 @@ SHARE = 4
 GROUPS = COORDS // SHARE
 QUADRANTS = 4
 SYNC_GROUPS = 5
-LATE = 2
+STORE_COLS = 256
+LATE = 4
+LAST = 2
 
 FLOPS = 2 * ROWS * COORDS * DPI * OUT
 
 
 def tile_positionencoder_k_kernel(tc, state, W_words, W_scales, b, gamma, beta, out):
     nc = tc.nc
+    starts = [sum(CHUNK_WIDTHS[:i]) for i in range(len(CHUNK_WIDTHS))]
+    chunk_cols = [slice(s, s + w) for s, w in zip(starts, CHUNK_WIDTHS)]
     with (
         tc.tile_pool(name="keep", bufs=1) as keep,
         tc.tile_pool(name="stage", bufs=2) as stage,
-        tc.psum_pool(name="spread_psum", bufs=CHUNKS) as spread_psum,
+        tc.psum_pool(name="spread_psum", bufs=CHUNKS - 1) as spread_psum,
         tc.psum_pool(name="vector_psum", bufs=2) as vector_psum,
         tc.psum_pool(name="acc_psum", bufs=1) as acc_psum,
     ):
@@ -85,11 +90,14 @@ def tile_positionencoder_k_kernel(tc, state, W_words, W_scales, b, gamma, beta, 
                 if g == 2:
                     for i, vector in enumerate((b, gamma, beta)):
                         nc.sync.dma_start(out=vector_rows[i : i + 1, :], in_=vector.unsqueeze(0))
-        late_words = W_words[COORDS - LATE : COORDS].rearrange("g p n t -> p g (n t)").bitcast(I32)
-        for half in range(HALVES):
-            cols = slice(BANK * half, BANK * (half + 1))
+        middle = COORDS - LAST
+        pieces = [(COORDS - LATE, middle, chunk_cols[0]), (middle, COORDS, chunk_cols[0])]
+        pieces.append((COORDS - LATE, middle, slice(CHUNK_WIDTHS[0], OUT)))
+        pieces.extend((middle, COORDS, cols) for cols in chunk_cols[1:])
+        for first, last, cols in pieces:
             nc.sync.dma_start(
-                out=w_words[:, COORDS - LATE : COORDS, cols].bitcast(I32), in_=late_words[:, :, cols]
+                out=w_words[:, first:last, cols].bitcast(I32),
+                in_=W_words[first:last].rearrange("g p n t -> p g (n t)").bitcast(I32)[:, :, cols],
             )
 
         cleared = keep.tile([P, INDEX_BITS, PACK], I32)
@@ -167,72 +175,87 @@ def tile_positionencoder_k_kernel(tc, state, W_words, W_scales, b, gamma, beta, 
             nc.vector.tensor_copy(out=vectors[:, i, :], in_=picked[:])
         b_all, gamma_all, beta_all = vectors[:, 0, :], vectors[:, 1, :], vectors[:, 2, :]
 
-        acc = [acc_psum.tile([ROWS, BANK], F32, name="acc%d" % half) for half in range(HALVES)]
-        early = [(g, half) for g in range(COORDS - LATE) for half in range(HALVES)]
-        late = [(g, half) for half in range(HALVES) for g in range(COORDS - LATE, COORDS)]
-        for g, half in early + late:
+        acc = [
+            acc_psum.tile([ROWS, width], F32, name="acc%d" % i) for i, width in enumerate(CHUNK_WIDTHS)
+        ]
+        early = [(g, i) for g in range(COORDS - LATE) for i in range(len(CHUNK_WIDTHS))]
+        late = [(g, 0) for g in range(COORDS - LATE, COORDS)]
+        for passes in (range(COORDS - LATE, middle), range(middle, COORDS)):
+            late.extend((g, i) for i in range(1, len(CHUNK_WIDTHS)) for g in passes)
+        for g, i in early + late:
             group, place = divmod(g, SHARE)
             rows = slice(ROWS * g, ROWS * (g + 1))
-            cols = slice(BANK * half, BANK * (half + 1))
             nc.tensor.matmul_mx(
-                out=acc[half][:],
+                out=acc[i][:],
                 lhsT=pe_codes[:, rows].bitcast(FP8X4),
                 lhsT_scale=pe_scales[:, rows],
-                rhs=w_words[:, g, cols].bitcast(FP8X4),
-                rhs_scale=w_planes[4 * place : P, group, cols],
+                rhs=w_words[:, g, chunk_cols[i]].bitcast(FP8X4),
+                rhs_scale=w_planes[4 * place : P, group, chunk_cols[i]],
                 start=(g == 0),
                 stop=(g == COORDS - 1),
             )
 
-        y = keep.tile([ROWS, OUT], F32)
-        squares = keep.tile([ROWS, OUT], F32)
-        sums = keep.tile([ROWS, HALVES], F32)
-        square_sums = [keep.tile([ROWS, 1], F32, name="square_sum%d" % half) for half in range(HALVES)]
-        minus_shift = keep.tile([ROWS, 1], F32)
-        for half in range(HALVES):
-            cols = slice(BANK * half, BANK * (half + 1))
-            nc.vector.scalar_tensor_tensor(
-                out=y[:, cols], in0=acc[half][:], scalar=1.0, in1=b_all[:, cols],
-                op0=ALU.mult, op1=ALU.add, accum_out=sums[:, half : half + 1],
+        with tc.manual_schedule(engines={mybir.EngineType.DVE, mybir.EngineType.Activation}):
+            y = keep.tile([ROWS, OUT], F32)
+            squares = keep.tile([ROWS, OUT], F32)
+            minus_shift = keep.tile([ROWS, 1], F32)
+            total = None
+            variance = eps
+            for i, cols in enumerate(chunk_cols):
+                chunk_sum = keep.tile([ROWS, 1], F32, name="chunk_sum%d" % i)
+                nc.vector.scalar_tensor_tensor(
+                    out=y[:, cols], in0=acc[i][:], scalar=1.0, in1=b_all[:, cols],
+                    op0=ALU.mult, op1=ALU.add, accum_out=chunk_sum[:],
+                )
+                last = i == len(chunk_cols) - 1
+                if i == 0:
+                    nc.vector.tensor_scalar_mul(out=minus_shift[:], in0=chunk_sum[:], scalar1=-1.0 / CHUNK_WIDTHS[0])
+                    total = chunk_sum
+                elif not last:
+                    new_total = keep.tile([ROWS, 1], F32, name="total%d" % i)
+                    nc.vector.tensor_scalar(
+                        out=new_total[:], in0=chunk_sum[:], scalar1=total[:], scalar2=None, op0=ALU.add,
+                    )
+                    total = new_total
+                square_sum = keep.tile([ROWS, 1], F32, name="square_sum%d" % i)
+                nc.scalar.activation(
+                    out=squares[:, cols], in_=y[:, cols], func=ACT.Square, bias=minus_shift[:], scale=1.0,
+                    accum_out=square_sum[:],
+                )
+                if not last:
+                    new_variance = keep.tile([ROWS, 1], F32, name="variance%d" % i)
+                    nc.scalar.activation(
+                        out=new_variance[:], in_=square_sum[:], func=ACT.Identity, bias=variance[:],
+                        scale=1.0 / OUT,
+                    )
+                    variance = new_variance
+            mean = keep.tile([ROWS, 1], F32)
+            nc.vector.tensor_scalar(
+                out=mean[:], in0=chunk_sum[:], scalar1=total[:], scalar2=1.0 / OUT, op0=ALU.add, op1=ALU.mult,
             )
-            if half == 0:
-                nc.vector.tensor_scalar_mul(out=minus_shift[:], in0=sums[:, 0:1], scalar1=-1.0 / BANK)
+            centred = keep.tile([ROWS, OUT], F32)
+            nc.vector.scalar_tensor_tensor(
+                out=centred[:], in0=y[:], scalar=mean[:], in1=gamma_all, op0=ALU.subtract, op1=ALU.mult,
+            )
+            offset_squared = keep.tile([ROWS, 1], F32)
             nc.scalar.activation(
-                out=squares[:, cols], in_=y[:, cols], func=ACT.Square, bias=minus_shift[:], scale=1.0,
-                accum_out=square_sums[half][:],
+                out=offset_squared[:], in_=mean[:], func=ACT.Square, bias=minus_shift[:], scale=1.0,
             )
-        mean = keep.tile([ROWS, 1], F32)
-        nc.vector.tensor_scalar(
-            out=mean[:], in0=sums[:, 0:1], scalar1=sums[:, 1:2], scalar2=1.0 / OUT,
-            op0=ALU.add, op1=ALU.mult,
-        )
-        centred = keep.tile([ROWS, OUT], F32)
-        nc.vector.scalar_tensor_tensor(
-            out=centred[:], in0=y[:], scalar=mean[:], in1=gamma_all, op0=ALU.subtract, op1=ALU.mult,
-        )
-        first_term = keep.tile([ROWS, 1], F32)
-        nc.scalar.activation(
-            out=first_term[:], in_=square_sums[0][:], func=ACT.Identity, bias=eps[:], scale=1.0 / OUT,
-        )
-        offset_squared = keep.tile([ROWS, 1], F32)
-        nc.scalar.activation(
-            out=offset_squared[:], in_=mean[:], func=ACT.Square, bias=minus_shift[:], scale=1.0,
-        )
-        other_terms = keep.tile([ROWS, 1], F32)
-        nc.scalar.activation(
-            out=other_terms[:], in_=offset_squared[:], func=ACT.Identity, bias=first_term[:], scale=-1.0,
-        )
-        std = keep.tile([ROWS, 1], F32)
-        nc.scalar.activation(
-            out=std[:], in_=square_sums[1][:], func=ACT.Sqrt, bias=other_terms[:], scale=1.0 / OUT,
-        )
-        rstd = keep.tile([ROWS, 1], F32)
-        nc.vector.reciprocal(out=rstd[:], in_=std[:])
-        result = keep.tile([ROWS, OUT], F32)
-        for half in range(HALVES):
-            cols = slice(BANK * half, BANK * (half + 1))
-            nc.vector.scalar_tensor_tensor(
-                out=result[:, cols], in0=centred[:, cols], scalar=rstd[:], in1=beta_all[:, cols],
-                op0=ALU.mult, op1=ALU.add,
+            other_terms = keep.tile([ROWS, 1], F32)
+            nc.scalar.activation(
+                out=other_terms[:], in_=offset_squared[:], func=ACT.Identity, bias=variance[:], scale=-1.0,
             )
-            nc.sync.dma_start(out=out[:, cols], in_=result[:, cols])
+            std = keep.tile([ROWS, 1], F32)
+            nc.scalar.activation(
+                out=std[:], in_=square_sum[:], func=ACT.Sqrt, bias=other_terms[:], scale=1.0 / OUT,
+            )
+            rstd = keep.tile([ROWS, 1], F32)
+            nc.vector.reciprocal(out=rstd[:], in_=std[:])
+            result = keep.tile([ROWS, OUT], F32)
+            for first in range(0, OUT, STORE_COLS):
+                cols = slice(first, first + STORE_COLS)
+                nc.vector.scalar_tensor_tensor(
+                    out=result[:, cols], in0=centred[:, cols], scalar=rstd[:], in1=beta_all[:, cols],
+                    op0=ALU.mult, op1=ALU.add,
+                )
+                nc.sync.dma_start(out=out[:, cols], in_=result[:, cols])

@@ -57,13 +57,8 @@ def tile_positionencoder_k_kernel(tc, state, W_words, W_scales, b, gamma, beta, 
         state_sb = keep.tile([ROWS, COORDS], BF16)
         nc.scalar.dma_start(out=state_sb[:], in_=state)
 
-        zero = keep.tile([P, 1], F32)
-        nc.vector.memset(zero[:], 0.0)
-        sin_warmer = keep.tile([P, 1], F32)
-        nc.scalar.activation(out=sin_warmer[:], in_=zero[:], func=ACT.Sin)
-
-        w_words = keep.tile([P, COORDS, OUT], U32, align_bytes=64)
-        w_planes = keep.tile([P, GROUPS, OUT], U8, align_bytes=64)
+        w_words = keep.tile([P, COORDS, OUT], U32, align_bytes=256)
+        w_planes = keep.tile([P, GROUPS, OUT], U8, align_bytes=256)
 
         def load_scale_rows(queue, view, group):
             first = SHARE * group
@@ -135,8 +130,8 @@ def tile_positionencoder_k_kernel(tc, state, W_words, W_scales, b, gamma, beta, 
             out=clipped[:], in0=state_sb[:], scalar1=0.0, scalar2=MAX_COORD,
             op0=ALU.max, op1=ALU.min,
         )
-        pe_codes = keep.tile([P, COORDS * ROWS], U32, align_bytes=64)
-        pe_scales = keep.tile([P, COORDS * ROWS], U8, align_bytes=64)
+        pe_codes = keep.tile([P, COORDS * ROWS], U32, align_bytes=256)
+        pe_scales = keep.tile([P, COORDS * ROWS], U8, align_bytes=256)
         for chunk in range(CHUNKS):
             spread = spread_psum.tile([P, CHUNK, ROWS], BF16)
             for i in range(CHUNK):
@@ -151,7 +146,7 @@ def tile_positionencoder_k_kernel(tc, state, W_words, W_scales, b, gamma, beta, 
                     out=planes[:, t, :], in_=spread[:].rearrange("p i r -> p (i r)"), func=ACT.Sin,
                     bias=phase[:, t : t + 1], scale=freq[:, t : t + 1],
                 )
-            grouped = stage.tile([P, CHUNK_COLS, PACK], BF16, align_bytes=64)
+            grouped = stage.tile([P, CHUNK_COLS, PACK], BF16, align_bytes=256)
             nc.vector.tensor_copy(out=grouped[:], in_=planes[:].rearrange("p t w -> p w t"))
             cols = slice(CHUNK_COLS * chunk, CHUNK_COLS * (chunk + 1))
             nc.vector.quantize_mx(
@@ -251,7 +246,7 @@ def tile_positionencoder_k_kernel(tc, state, W_words, W_scales, b, gamma, beta, 
             )
             rstd = keep.tile([ROWS, 1], F32)
             nc.vector.reciprocal(out=rstd[:], in_=std[:])
-            result = keep.tile([ROWS, OUT], F32)
+            result = keep.tile([ROWS, OUT], F32, align_bytes=256)
             for first in range(0, OUT, STORE_COLS):
                 cols = slice(first, first + STORE_COLS)
                 nc.vector.scalar_tensor_tensor(

@@ -32,6 +32,7 @@ GROUPS = COORDS // SHARE
 QUADRANTS = 4
 SYNC_GROUPS = 5
 STORE_COLS = 256
+WORD_RUNS = (1, 1, 2) + 5 * (4,) + (2, 2)
 LATE = 4
 LAST = 2
 
@@ -74,17 +75,18 @@ def tile_positionencoder_k_kernel(tc, state, W_words, W_scales, b, gamma, beta, 
         nc.vector.memset(vector_rows[:].bitcast(I32), 0)
         for group in range(SYNC_GROUPS, GROUPS):
             load_scale_rows(nc.gpsimd, F32, group)
-        for group in range(GROUPS):
-            for g in range(SHARE * group, min(SHARE * (group + 1), COORDS - LATE)):
-                nc.sync.dma_start(
-                    out=w_words[:, g, :].bitcast(I32),
-                    in_=W_words[g].rearrange("p n t -> p (n t)").bitcast(I32),
-                )
-                if g == SHARE * group and group < SYNC_GROUPS:
-                    load_scale_rows(nc.sync, I32, group)
-                if g == 2:
-                    for i, vector in enumerate((b, gamma, beta)):
-                        nc.sync.dma_start(out=vector_rows[i : i + 1, :], in_=vector.unsqueeze(0))
+        g = 0
+        for run in WORD_RUNS:
+            nc.sync.dma_start(
+                out=w_words[:, g : g + run, :].bitcast(I32),
+                in_=W_words[g : g + run].rearrange("g p n t -> p g (n t)").bitcast(I32),
+            )
+            if g % SHARE == 0 and g // SHARE < SYNC_GROUPS:
+                load_scale_rows(nc.sync, I32, g // SHARE)
+            if g == 2:
+                for i, vector in enumerate((b, gamma, beta)):
+                    nc.sync.dma_start(out=vector_rows[i : i + 1, :], in_=vector.unsqueeze(0))
+            g += run
         middle = COORDS - LAST
         pieces = [(COORDS - LATE, middle, chunk_cols[0]), (middle, COORDS, chunk_cols[0])]
         pieces.append((COORDS - LATE, middle, slice(CHUNK_WIDTHS[0], OUT)))

import math

import concourse.masks as masks
import concourse.mybir as mybir

F32 = mybir.dt.float32
BF16 = mybir.dt.bfloat16
I32 = mybir.dt.int32
U32 = mybir.dt.uint32
U8 = mybir.dt.uint8
FP8X4 = mybir.dt.float8_e4m3fn_x4
ALU = mybir.AluOpType
ACT = mybir.ActivationFunctionType

P = 128
PACK = 4
ROWS = 128
COORDS = 32
DPI = P * PACK
OUT = 1024
BANK = 512
HALVES = OUT // BANK
CHUNK_WIDTHS = (512, 256, 256)
MAX_COORD = 10.0
LN_EPS = 1e-5
INDEX_BITS = 9
CHUNK = 8
CHUNKS = COORDS // CHUNK
CHUNK_COLS = CHUNK * ROWS
SHARE = 4
GROUPS = COORDS // SHARE
QUADRANTS = 4
SYNC_GROUPS = 5
STORE_COLS = 256
WORD_RUNS = (1, 1, 2) + 5 * (4,) + (2, 2)
LATE = 4
LAST = 2

FLOPS = 2 * ROWS * COORDS * DPI * OUT


def tile_positionencoder_k_kernel(tc, state, W_words, W_scales, b, gamma, beta, out):
    nc = tc.nc
    starts = [sum(CHUNK_WIDTHS[:i]) for i in range(len(CHUNK_WIDTHS))]
    chunk_cols = [slice(s, s + w) for s, w in zip(starts, CHUNK_WIDTHS)]
    with (
        tc.tile_pool(name="keep", bufs=1) as keep,
        tc.tile_pool(name="stage", bufs=2) as stage,
        tc.psum_pool(name="spread_psum", bufs=CHUNKS - 1) as spread_psum,
        tc.psum_pool(name="vector_psum", bufs=2) as vector_psum,
        tc.psum_pool(name="acc_psum", bufs=1) as acc_psum,
    ):
        identity = keep.tile([P, P], BF16)
        masks.make_identity(nc, identity[:])
        not_j = keep.tile([P, PACK], I32)
        nc.gpsimd.iota(not_j[:], pattern=[[-1, PACK]], base=DPI - 1, channel_multiplier=-PACK)

        state_sb = keep.tile([ROWS, COORDS], BF16)
        nc.scalar.dma_start(out=state_sb[:], in_=state)

        w_words = keep.tile([P, COORDS, OUT], U32, align_bytes=256)
        w_planes = keep.tile([P, GROUPS, OUT], U8, align_bytes=256)

        def load_scale_rows(queue, view, group):
            first = SHARE * group
            for quadrant in range(QUADRANTS):
                queue.dma_start(
                    out=w_planes[32 * quadrant : 32 * quadrant + 4 * SHARE, group, :].bitcast(view),
                    in_=W_scales[first : first + SHARE, 4 * quadrant : 4 * quadrant + 4, :].bitcast(view),
                )

        for group in [0, *range(SYNC_GROUPS, GROUPS), *range(1, SYNC_GROUPS)]:
            nc.vector.memset(w_planes[:, group, :].bitcast(I32), 0)
        vector_rows = keep.tile([P, OUT], BF16)
        nc.vector.memset(vector_rows[:].bitcast(I32), 0)
        for group in range(SYNC_GROUPS, GROUPS):
            load_scale_rows(nc.gpsimd, F32, group)
        g = 0
        for run in WORD_RUNS:
            nc.sync.dma_start(
                out=w_words[:, g : g + run, :].bitcast(I32),
                in_=W_words[g : g + run].rearrange("g p n t -> p g (n t)").bitcast(I32),
            )
            if g % SHARE == 0 and g // SHARE < SYNC_GROUPS:
                load_scale_rows(nc.sync, I32, g // SHARE)
            if g == 2:
                for i, vector in enumerate((b, gamma, beta)):
                    nc.sync.dma_start(out=vector_rows[i : i + 1, :], in_=vector.unsqueeze(0))
            g += run
        middle = COORDS - LAST
        pieces = [(COORDS - LATE, middle, chunk_cols[0]), (middle, COORDS, chunk_cols[0])]
        pieces.append((COORDS - LATE, middle, slice(CHUNK_WIDTHS[0], OUT)))
        pieces.extend((middle, COORDS, cols) for cols in chunk_cols[1:])
        for first, last, cols in pieces:
            nc.sync.dma_start(
                out=w_words[:, first:last, cols].bitcast(I32),
                in_=W_words[first:last].rearrange("g p n t -> p g (n t)").bitcast(I32)[:, :, cols],
            )

        cleared = keep.tile([P, INDEX_BITS, PACK], I32)
        factors = keep.tile([P, INDEX_BITS, PACK], F32)
        for i in range(INDEX_BITS):
            ratio = 10000.0 ** (-2.0 * (1 << i) / DPI)
            nc.vector.tensor_scalar(
                out=cleared[:, i, :], in0=not_j[:], scalar1=i, scalar2=1,
                op0=ALU.logical_shift_right, op1=ALU.bitwise_and,
            )
            nc.vector.tensor_scalar(
                out=factors[:, i, :], in0=cleared[:, i, :], scalar1=1.0 - ratio, scalar2=ratio,
                op0=ALU.mult, op1=ALU.add,
            )
        f_of_j = keep.tile([P, PACK], F32)
        nc.vector.tensor_reduce(
            out=f_of_j[:], in_=factors[:].rearrange("p i t -> p t i"),
            axis=mybir.AxisListType.X, op=ALU.mult,
        )
        freq = keep.tile([P, PACK], F32)
        nc.vector.tensor_scalar_mul(out=freq[:], in0=f_of_j[:], scalar1=1.0 / MAX_COORD)
        phase = keep.tile([P, PACK], F32)
        nc.vector.tensor_scalar(
            out=phase[:], in0=cleared[:, 0, :], scalar1=-math.pi / 2, scalar2=math.pi / 2,
            op0=ALU.mult, op1=ALU.add,
        )
        eps = keep.tile([P, 1], F32)
        nc.vector.tensor_scalar(
            out=eps[:], in0=cleared[:, 0, 0:1], scalar1=0.0, scalar2=LN_EPS,
            op0=ALU.mult, op1=ALU.add,
        )

        clipped = keep.tile([ROWS, COORDS], BF16)
        nc.vector.tensor_scalar(
            out=clipped[:], in0=state_sb[:], scalar1=0.0, scalar2=MAX_COORD,
            op0=ALU.max, op1=ALU.min,
        )
        pe_codes = keep.tile([P, COORDS * ROWS], U32, align_bytes=256)
        pe_scales = keep.tile([P, COORDS * ROWS], U8, align_bytes=256)
        for chunk in range(CHUNKS):
            spread = spread_psum.tile([P, CHUNK, ROWS], BF16)
            for i in range(CHUNK):
                c = CHUNK * chunk + i
                nc.tensor.matmul(
                    out=spread[:, i, :], lhsT=clipped[:, c : c + 1].to_broadcast([ROWS, P]),
                    rhs=identity[:], start=True, stop=True,
                )
            planes = stage.tile([P, PACK, CHUNK_COLS], BF16)
            for t in range(PACK):
                nc.scalar.activation(
                    out=planes[:, t, :], in_=spread[:].rearrange("p i r -> p (i r)"), func=ACT.Sin,
                    bias=phase[:, t : t + 1], scale=freq[:, t : t + 1],
                )
            grouped = stage.tile([P, CHUNK_COLS, PACK], BF16, align_bytes=256)
            nc.vector.tensor_copy(out=grouped[:], in_=planes[:].rearrange("p t w -> p w t"))
            cols = slice(CHUNK_COLS * chunk, CHUNK_COLS * (chunk + 1))
            nc.vector.quantize_mx(
                out=pe_codes[:, cols].bitcast(FP8X4), scales=pe_scales[:, cols],
                in_=grouped[:].rearrange("p w t -> p (w t)"),
            )
        table_warmer = keep.tile([P, 1], F32)
        nc.scalar.activation(
            out=table_warmer[:], in_=planes[:, PACK - 1, 0:1], func=ACT.Sqrt, bias=eps[:], scale=0.0,
        )

        vectors = keep.tile([P, 3, OUT], BF16)
        for i in range(3):
            picked = vector_psum.tile([P, OUT], BF16)
            for half in range(HALVES):
                cols = slice(BANK * half, BANK * (half + 1))
                nc.tensor.matmul(
                    out=picked[:, cols], lhsT=identity[:, i : i + 1].to_broadcast([P, P]),
                    rhs=vector_rows[:, cols], start=True, stop=True,
                )
            nc.vector.tensor_copy(out=vectors[:, i, :], in_=picked[:])
        b_all, gamma_all, beta_all = vectors[:, 0, :], vectors[:, 1, :], vectors[:, 2, :]

        acc = [
            acc_psum.tile([ROWS, width], F32, name="acc%d" % i) for i, width in enumerate(CHUNK_WIDTHS)
        ]
        early = [(g, i) for g in range(COORDS - LATE) for i in range(len(CHUNK_WIDTHS))]
        late = [(g, 0) for g in range(COORDS - LATE, COORDS)]
        for passes in (range(COORDS - LATE, middle), range(middle, COORDS)):
            late.extend((g, i) for i in range(1, len(CHUNK_WIDTHS)) for g in passes)
        for g, i in early + late:
            group, place = divmod(g, SHARE)
            rows = slice(ROWS * g, ROWS * (g + 1))
            nc.tensor.matmul_mx(
                out=acc[i][:],
                lhsT=pe_codes[:, rows].bitcast(FP8X4),
                lhsT_scale=pe_scales[:, rows],
                rhs=w_words[:, g, chunk_cols[i]].bitcast(FP8X4),
                rhs_scale=w_planes[4 * place : P, group, chunk_cols[i]],
                start=(g == 0),
                stop=(g == COORDS - 1),
            )

        with tc.manual_schedule(engines={mybir.EngineType.DVE, mybir.EngineType.Activation}):
            y = keep.tile([ROWS, OUT], F32)
            squares = keep.tile([ROWS, OUT], F32)
            minus_shift = keep.tile([ROWS, 1], F32)
            total = None
            variance = eps
            for i, cols in enumerate(chunk_cols):
                chunk_sum = keep.tile([ROWS, 1], F32, name="chunk_sum%d" % i)
                nc.vector.scalar_tensor_tensor(
                    out=y[:, cols], in0=acc[i][:], scalar=1.0, in1=b_all[:, cols],
                    op0=ALU.mult, op1=ALU.add, accum_out=chunk_sum[:],
                )
                last = i == len(chunk_cols) - 1
                if i == 0:
                    nc.vector.tensor_scalar_mul(out=minus_shift[:], in0=chunk_sum[:], scalar1=-1.0 / CHUNK_WIDTHS[0])
                    total = chunk_sum
                elif not last:
                    new_total = keep.tile([ROWS, 1], F32, name="total%d" % i)
                    nc.vector.tensor_scalar(
                        out=new_total[:], in0=chunk_sum[:], scalar1=total[:], scalar2=None, op0=ALU.add,
                    )
                    total = new_total
                square_sum = keep.tile([ROWS, 1], F32, name="square_sum%d" % i)
                nc.scalar.activation(
                    out=squares[:, cols], in_=y[:, cols], func=ACT.Square, bias=minus_shift[:], scale=1.0,
                    accum_out=square_sum[:],
                )
                if not last:
                    new_variance = keep.tile([ROWS, 1], F32, name="variance%d" % i)
                    nc.scalar.activation(
                        out=new_variance[:], in_=square_sum[:], func=ACT.Identity, bias=variance[:],
                        scale=1.0 / OUT,
                    )
                    variance = new_variance
            mean = keep.tile([ROWS, 1], F32)
            nc.vector.tensor_scalar(
                out=mean[:], in0=chunk_sum[:], scalar1=total[:], scalar2=1.0 / OUT, op0=ALU.add, op1=ALU.mult,
            )
            centred = keep.tile([ROWS, OUT], F32)
            nc.vector.scalar_tensor_tensor(
                out=centred[:], in0=y[:], scalar=mean[:], in1=gamma_all, op0=ALU.subtract, op1=ALU.mult,
            )
            offset_squared = keep.tile([ROWS, 1], F32)
            nc.scalar.activation(
                out=offset_squared[:], in_=mean[:], func=ACT.Square, bias=minus_shift[:], scale=1.0,
            )
            other_terms = keep.tile([ROWS, 1], F32)
            nc.scalar.activation(
                out=other_terms[:], in_=offset_squared[:], func=ACT.Identity, bias=variance[:], scale=-1.0,
            )
            std = keep.tile([ROWS, 1], F32)
            nc.scalar.activation(
                out=std[:], in_=square_sum[:], func=ACT.Sqrt, bias=other_terms[:], scale=1.0 / OUT,
            )
            rstd = keep.tile([ROWS, 1], F32)
            nc.vector.reciprocal(out=rstd[:], in_=std[:])
            result = keep.tile([ROWS, OUT], F32, align_bytes=256)
            for first in range(0, OUT, STORE_COLS):
                cols = slice(first, first + STORE_COLS)
                nc.vector.scalar_tensor_tensor(
                    out=result[:, cols], in0=centred[:, cols], scalar=rstd[:], in1=beta_all[:, cols],
                    op0=ALU.mult, op1=ALU.add,
                )
                nc.sync.dma_start(out=out[:, cols], in_=result[:, cols])
